import numpy as np
import ml_dtypes


def mxq(x, axis, fmt="e4m3"):
    dtype, down = {"e4m3": (ml_dtypes.float8_e4m3fn, 7), "e5m2": (ml_dtypes.float8_e5m2, 14)}[fmt]
    v = np.moveaxis(np.asarray(x, np.float32).astype(ml_dtypes.bfloat16).astype(np.float64), axis, -1)
    blocks = v.reshape(v.shape[:-1] + (-1, 32))
    amax = np.abs(blocks).max(-1, keepdims=True)
    byte = np.maximum(np.where(amax > 0, np.frexp(amax)[1] - 1 + 127, 0) - down, 1)
    scale = np.exp2(byte - 127.0)
    codes = (blocks / scale).astype(np.float32).astype(dtype).astype(np.float64)
    return np.moveaxis((codes * scale).reshape(v.shape), -1, axis)


WIDE = False


def mx_kscale(k):
    if not WIDE:
        return np.ones(k)
    levels = np.array([10, -10, 5, -5, 0])
    a = np.random.permutation(np.resize(levels, k // 512 * 4)).reshape(k // 512, 4)
    idx = np.arange(k)
    return np.exp2(a[idx // 512, idx % 128 // 32])


BF16 = ml_dtypes.bfloat16


def bf(x):
    return np.asarray(x, np.float32).astype(BF16)


def f64(x):
    return np.asarray(x).astype(np.float64)


B, F, M, N, H, O = 1, 128, 128, 128, 512, 128
BN_EPS = 1e-5
COS_EPS = 1e-8


def bn(x, g, b, m, v):
    sh = [1] * x.ndim
    sh[1] = -1
    return g.reshape(sh) * (x - m.reshape(sh)) * (1.0 / np.sqrt(v.reshape(sh) + BN_EPS)) + b.reshape(sh)


def setup_inputs():
    k = mx_kscale(H)
    w1 = np.random.standard_normal((H, F + 1)) * 0.7 / np.sqrt(F)
    w1[:, 0] *= F
    return {"template_feature": bf(np.random.standard_normal((B, F, M))),
            "search_feature": bf(np.random.standard_normal((B, F, N))),
            "W1": bf(w1),
            "W2": bf(np.random.standard_normal((H, H)) * 1.4 / np.sqrt(H) / k[None, :]),
            "g1": bf((1.0 + 0.1 * np.random.standard_normal(H)) * k),
            "b1": bf(0.2 * np.random.standard_normal(H) * k),
            "m1": bf(0.2 * np.random.standard_normal(H)),
            "v1": bf(np.random.uniform(0.5, 1.5, H)),
            "g2": bf(1.0 + 0.1 * np.random.standard_normal(H)),
            "b2": bf(0.2 * np.random.standard_normal(H)),
            "m2": bf(0.2 * np.random.standard_normal(H)),
            "v2": bf(np.random.uniform(0.5, 1.5, H))}


def reference(template_feature, search_feature, W1, W2, g1, b1, m1, v1, g2, b2, m2, v2):
    t, s = f64(template_feature), f64(search_feature)
    dot = f64(template_feature).transpose(0, 2, 1) @ f64(search_feature)
    nt = np.sqrt((t * t).sum(1))
    ns = np.sqrt((s * s).sum(1))
    cos = dot / np.maximum(nt[:, :, None] * ns[:, None, :], COS_EPS)
    a = (f64(W1)[:, 1:] @ f64(template_feature))[..., None] + f64(W1)[:, 0][None, :, None, None] * cos[:, None]
    h1 = np.maximum(bn(a, f64(g1), f64(b1), f64(m1), f64(v1)), 0.0)
    x2 = (mxq(f64(W2), 1, "e4m3") @ mxq(h1.reshape(B, H, M * N), 1, "e4m3")).reshape(B, H, M, N)
    return np.maximum(bn(x2, f64(g2), f64(b2), f64(m2), f64(v2)), 0.0)

@@ -1,0 +1,266 @@
+from contextlib import ExitStack
+
+import concourse.mybir as mybir
+from concourse.masks import make_identity
+
+F32 = mybir.dt.float32
+BF16 = mybir.dt.bfloat16
+U32 = mybir.dt.uint32
+U8 = mybir.dt.uint8
+FP8X4 = mybir.dt.float8_e4m3fn_x4
+ALU = mybir.AluOpType
+ACT = mybir.ActivationFunctionType
+
+P = 128
+PACK = 4
+F = 128
+M = 128
+N = 128
+H = P * PACK
+BN_EPS = 1e-5
+COS_EPS = 1e-8
+TINY = 1e-30
+
+M_UNIT = 4
+COLS = M_UNIT * N
+UNITS = M // M_UNIT
+
+FLOPS = 2 * H * H * M * N + 2 * F * M * N + 2 * H * F * M
+
+
+def tile_p2b_xcorr_pa_kernel(
+    tc, template_feature, search_feature, W1, W2, g1, b1, m1, v1, g2, b2, m2, v2, out
+):
+    nc = tc.nc
+    out_rows = out[0, :, :, :].rearrange("(p j) m n -> p j (m n)", j=PACK)
+
+    with ExitStack() as ctx:
+        ctx.enter_context(tc.manual_schedule())
+        const = ctx.enter_context(tc.tile_pool(name="const", bufs=1))
+        work = ctx.enter_context(tc.tile_pool(name="work", bufs=3))
+        store = ctx.enter_context(tc.tile_pool(name="store", bufs=4))
+        cos_psum = ctx.enter_context(tc.psum_pool(name="cos_psum", bufs=2))
+        acc_psum = ctx.enter_context(tc.psum_pool(name="acc_psum", bufs=6))
+
+        t_sb = const.tile([F, M], BF16, name="t_sb")
+        nc.sync.dma_start(out=t_sb[:], in_=template_feature[0, :, :])
+        s_sb = const.tile([F, N], BF16, name="s_sb")
+        nc.scalar.dma_start(out=s_sb[:], in_=search_feature[0, :, :])
+        w2_sb = const.tile([P, PACK * H], BF16, name="w2_sb")
+        nc.scalar.dma_start(out=w2_sb[:], in_=W2.rearrange("(p j) h -> p (j h)", j=PACK))
+
+        VAR, GAIN, MEAN, SHIFT = 0, 1, 2, 3
+        bn_in = const.tile([P, 2, 4, 16], BF16, name="bn_in")
+
+        def load_bn(vector, layer, kind):
+            nc.sync.dma_start(
+                out=bn_in[:, layer, kind, 0:PACK], in_=vector.rearrange("(p j) -> p j", j=PACK)
+            )
+
+        load_bn(v1, 0, VAR)
+        load_bn(v2, 1, VAR)
+        w1_sb = const.tile([P, PACK, F + 1], BF16, name="w1_sb")
+        nc.sync.dma_start(out=w1_sb[:], in_=W1.rearrange("(p j) c -> p j c", j=PACK))
+        load_bn(g1, 0, GAIN)
+        load_bn(m1, 0, MEAN)
+        load_bn(b1, 0, SHIFT)
+        load_bn(g2, 1, GAIN)
+        load_bn(m2, 1, MEAN)
+        load_bn(b2, 1, SHIFT)
+
+        ident_bf = const.tile([P, P], BF16, name="ident_bf")
+        make_identity(nc, ident_bf[:])
+        ident_f32 = const.tile([P, P], F32, name="ident_f32")
+        make_identity(nc, ident_f32[:])
+        ones = const.tile([P, P], F32, name="ones")
+        nc.vector.memset(ones[:], 1.0)
+        warm = const.tile([P, 1], F32, name="warm")
+        nc.scalar.activation(out=warm[:], in_=ones[:, 0:1], func=ACT.Abs_reciprocal_sqrt)
+
+        t_sq = const.tile([F, M], F32, name="t_sq")
+        nc.vector.tensor_tensor(out=t_sq[:], in0=t_sb[:], in1=t_sb[:], op=ALU.mult)
+        s_sq = const.tile([F, N], F32, name="s_sq")
+        nc.scalar.activation(out=s_sq[:], in_=s_sb[:], func=ACT.Square)
+
+        dot_ps = cos_psum.tile([N, M], F32, name="dot_ps", tag="bank")
+        nc.tensor.matmul(out=dot_ps[:], lhsT=s_sb[:], rhs=t_sb[:], start=True, stop=True)
+        norm_ps = cos_psum.tile([N, M + 1], F32, name="norm_ps", tag="bank")
+        nc.tensor.matmul(out=norm_ps[:, 0:M], lhsT=ones[:], rhs=t_sq[:], start=True, stop=True)
+        nc.tensor.matmul(
+            out=norm_ps[:, M : M + 1], lhsT=s_sq[:], rhs=ones[:, 0:1], start=True, stop=True
+        )
+
+        BN0 = M + 1
+        ROOTS = BN0 + 2 * PACK
+        x = const.tile([P, ROOTS], F32, name="x")
+        nc.vector.tensor_scalar_max(out=x[:, 0:BN0], in0=norm_ps[:], scalar1=TINY)
+        nc.vector.tensor_scalar_add(
+            out=x[:, BN0:ROOTS].rearrange("p (l j) -> p l j", j=PACK),
+            in0=bn_in[:, :, VAR, 0:PACK],
+            scalar1=BN_EPS,
+        )
+        r0 = const.tile([P, ROOTS], F32, name="r0")
+        nc.scalar.activation(out=r0[:], in_=x[:], func=ACT.Abs_reciprocal_sqrt)
+
+        w1t_ps = acc_psum.tile([F, PACK, P], BF16, name="w1t_ps", tag="bank")
+        for j in range(PACK):
+            nc.tensor.transpose(w1t_ps[:, j, :], w1_sb[:, j, 1 : F + 1], ident_bf[:])
+        w1t = const.tile([F, PACK, P], BF16, name="w1t")
+        nc.scalar.copy(out=w1t[:], in_=w1t_ps[:])
+
+        w2_words = w2_sb[:].bitcast(F32).rearrange("p (j q u) -> p j u q", j=PACK, u=2)
+        w2_grouped = const.tile([P, PACK * P * PACK], BF16, name="w2_grouped", align_bytes=64)
+        w2_grouped_words = w2_grouped[:].bitcast(F32).rearrange("p (j g u) -> p j g u", j=PACK, u=2)
+        for half in range(2):
+            w2t_ps = acc_psum.tile([P, 2, 2, P], F32, name="w2t_ps", tag="bank")
+            for jj in range(2):
+                for u in range(2):
+                    nc.tensor.transpose(
+                        w2t_ps[:, jj, u, :], w2_words[:, 2 * half + jj, u, :], ident_f32[:]
+                    )
+            nc.scalar.copy(
+                out=w2_grouped_words[:, 2 * half : 2 * half + 2, :, :],
+                in_=w2t_ps[:].rearrange("p j u g -> p j g u"),
+            )
+
+        u_ps = acc_psum.tile([P, PACK, M], F32, name="u_ps", tag="bank")
+        for j in range(PACK):
+            nc.tensor.matmul(out=u_ps[:, j, :], lhsT=w1t[:, j, :], rhs=t_sb[:], start=True, stop=True)
+
+        xr = const.tile([P, ROOTS], F32, name="xr")
+        nc.vector.tensor_tensor(out=xr[:], in0=x[:], in1=r0[:], op=ALU.mult)
+        half_xrr = const.tile([P, ROOTS], F32, name="half_xrr")
+        nc.vector.scalar_tensor_tensor(
+            out=half_xrr[:], in0=xr[:], scalar=-0.5, in1=r0[:], op0=ALU.mult, op1=ALU.mult
+        )
+        rs = const.tile([P, ROOTS], F32, name="rs")
+        nc.vector.scalar_tensor_tensor(
+            out=rs[:], in0=half_xrr[:], scalar=1.5, in1=r0[:], op0=ALU.add, op1=ALU.mult
+        )
+
+        inv = const.tile([N, M], F32, name="inv")
+        nc.vector.tensor_scalar(
+            out=inv[:], in0=rs[:, 0:M], scalar1=rs[:, M : M + 1], scalar2=1.0 / COS_EPS,
+            op0=ALU.mult, op1=ALU.min,
+        )
+        cos_t = const.tile([N, M], F32, name="cos_t")
+        nc.vector.tensor_tensor(out=cos_t[:], in0=inv[:], in1=dot_ps[:], op=ALU.mult)
+
+        def spread_cos(unit):
+            cos_ps = cos_psum.tile([P, M_UNIT, N], F32, name="cos_ps", tag="bank")
+            for i in range(M_UNIT):
+                m = unit * M_UNIT + i
+                nc.tensor.transpose(
+                    cos_ps[:, i, :], cos_t[:, m : m + 1].to_broadcast([N, P]), ident_f32[:]
+                )
+            return cos_ps
+
+        def copy_cos(cos_ps):
+            cos_sb = work.tile([P, M_UNIT, N], F32, name="cos_sb")
+            nc.scalar.copy(out=cos_sb[:], in_=cos_ps[:])
+            return cos_sb
+
+        def first_layer(unit, cos_sb):
+            a_bf = work.tile([P, PACK, COLS], BF16, name="a_bf")
+            for i in range(M_UNIT):
+                m = unit * M_UNIT + i
+                for j in range(PACK):
+                    nc.vector.tensor_scalar(
+                        out=a_bf[:, j, i * N : (i + 1) * N], in0=cos_sb[:, i, :],
+                        scalar1=c[:, j : j + 1], scalar2=base[:, j, m : m + 1],
+                        op0=ALU.mult, op1=ALU.add,
+                    )
+            return a_bf
+
+        def relu_and_group(a_bf):
+            grouped = work.tile([P, COLS * PACK], BF16, name="grouped", align_bytes=64)
+            nc.vector.tensor_scalar_max(
+                out=grouped[:].rearrange("p (c i t) -> p c t i", i=4, t=PACK),
+                in0=a_bf[:].rearrange("p t (c i) -> p c t i", i=4),
+                scalar1=0.0,
+            )
+            return grouped
+
+        def quantise(grouped):
+            codes = work.tile([P, COLS], U32, name="codes", align_bytes=64)
+            scales = work.tile([P, COLS], U8, name="scales", align_bytes=64)
+            nc.vector.quantize_mx(out=codes[:].bitcast(FP8X4), scales=scales[:], in_=grouped[:])
+            return codes, scales
+
+        def second_layer(codes, scales):
+            accs = []
+            for j in range(PACK):
+                acc = acc_psum.tile([P, COLS], F32, name="acc", tag="bank")
+                nc.tensor.matmul_mx(
+                    out=acc[:],
+                    lhsT=w2_codes[:, j * P : (j + 1) * P].bitcast(FP8X4),
+                    lhsT_scale=w2_scales[:, j * P : (j + 1) * P],
+                    rhs=codes[:].bitcast(FP8X4),
+                    rhs_scale=scales[:],
+                    start=True,
+                    stop=True,
+                )
+                accs.append(acc)
+            return accs
+
+        def finish(unit, accs):
+            result = store.tile([P, PACK, COLS], F32, name="result")
+            for j in range(PACK):
+                nc.scalar.activation(
+                    out=result[:, j, :], in_=accs[j][:], func=ACT.Relu,
+                    scale=bn_scale[:, 1, j : j + 1], bias=bn_shift[:, 1, j : j + 1],
+                )
+            nc.sync.dma_start(out=out_rows[:, :, unit * COLS : (unit + 1) * COLS], in_=result[:])
+
+        cos_ps0 = spread_cos(0)
+        cos_ps1 = spread_cos(1)
+        cos_sbs = {0: copy_cos(cos_ps0)}
+
+        bn_scale = const.tile([P, 2, PACK], F32, name="bn_scale")
+        bn_mean = const.tile([P, 2, PACK], F32, name="bn_mean")
+        bn_shift = const.tile([P, 2, PACK], F32, name="bn_shift")
+
+        def fold_bn(layer):
+            nc.vector.tensor_tensor(
+                out=bn_scale[:, layer, :], in0=bn_in[:, layer, GAIN, 0:PACK],
+                in1=rs[:, BN0 + layer * PACK : BN0 + (layer + 1) * PACK], op=ALU.mult,
+            )
+            nc.vector.tensor_tensor(
+                out=bn_mean[:, layer, :], in0=bn_scale[:, layer, :],
+                in1=bn_in[:, layer, MEAN, 0:PACK], op=ALU.mult,
+            )
+            nc.vector.tensor_tensor(
+                out=bn_shift[:, layer, :], in0=bn_in[:, layer, SHIFT, 0:PACK],
+                in1=bn_mean[:, layer, :], op=ALU.subtract,
+            )
+
+        fold_bn(0)
+        c = const.tile([P, PACK], F32, name="c")
+        nc.vector.tensor_tensor(out=c[:], in0=bn_scale[:, 0, :], in1=w1_sb[:, :, 0], op=ALU.mult)
+        base = const.tile([P, PACK, M], F32, name="base")
+        for j in range(PACK):
+            nc.scalar.activation(
+                out=base[:, j, :], in_=u_ps[:, j, :], func=ACT.Identity,
+                scale=bn_scale[:, 0, j : j + 1], bias=bn_shift[:, 0, j : j + 1],
+            )
+        cos_sbs[1] = copy_cos(cos_ps1)
+
+        w2_codes = const.tile([P, PACK * P], U32, name="w2_codes", align_bytes=64)
+        w2_scales = const.tile([P, PACK * P], U8, name="w2_scales", align_bytes=64)
+        nc.vector.quantize_mx(
+            out=w2_codes[:].bitcast(FP8X4), scales=w2_scales[:], in_=w2_grouped[:]
+        )
+        fold_bn(1)
+
+        a_bfs = {0: first_layer(0, cos_sbs[0])}
+        for unit in range(UNITS):
+            grouped = relu_and_group(a_bfs[unit])
+            if unit + 1 < UNITS:
+                a_bfs[unit + 1] = first_layer(unit + 1, cos_sbs[unit + 1])
+            codes, scales = quantise(grouped)
+            if unit + 2 < UNITS:
+                cos_ps = spread_cos(unit + 2)
+            accs = second_layer(codes, scales)
+            if unit + 2 < UNITS:
+                cos_sbs[unit + 2] = copy_cos(cos_ps)
+            finish(unit, accs)

@@ -24,6 +24,8 @@ TINY = 1e-30
 M_UNIT = 4
 COLS = M_UNIT * N
 UNITS = M // M_UNIT
+PIECES = M_UNIT * PACK
+SCALAR_PIECES = 1
 
 FLOPS = 2 * H * H * M * N + 2 * F * M * N + 2 * H * F * M
 
@@ -160,17 +162,26 @@ def tile_p2b_xcorr_pa_kernel(
             nc.scalar.copy(out=cos_sb[:], in_=cos_ps[:])
             return cos_sb
 
-        def first_layer(unit, cos_sb):
+        def first_layer_scalar(unit, cos_ps):
             a_bf = work.tile([P, PACK, COLS], BF16, name="a_bf")
-            for i in range(M_UNIT):
+            for piece in range(PIECES - SCALAR_PIECES, PIECES):
+                i, j = divmod(piece, PACK)
                 m = unit * M_UNIT + i
-                for j in range(PACK):
-                    nc.vector.tensor_scalar(
-                        out=a_bf[:, j, i * N : (i + 1) * N], in0=cos_sb[:, i, :],
-                        scalar1=c[:, j : j + 1], scalar2=base[:, j, m : m + 1],
-                        op0=ALU.mult, op1=ALU.add,
-                    )
+                nc.scalar.activation(
+                    out=a_bf[:, j, i * N : (i + 1) * N], in_=cos_ps[:, i, :], func=ACT.Identity,
+                    scale=c[:, j : j + 1], bias=base[:, j, m : m + 1],
+                )
             return a_bf
+
+        def first_layer_vector(unit, cos_sb, a_bf):
+            for piece in range(PIECES - SCALAR_PIECES):
+                i, j = divmod(piece, PACK)
+                m = unit * M_UNIT + i
+                nc.vector.tensor_scalar(
+                    out=a_bf[:, j, i * N : (i + 1) * N], in0=cos_sb[:, i, :],
+                    scalar1=c[:, j : j + 1], scalar2=base[:, j, m : m + 1],
+                    op0=ALU.mult, op1=ALU.add,
+                )
 
         def relu_and_group(a_bf):
             grouped = work.tile([P, COLS * PACK], BF16, name="grouped", align_bytes=64)
@@ -243,7 +254,9 @@ def tile_p2b_xcorr_pa_kernel(
                 out=base[:, j, :], in_=u_ps[:, j, :], func=ACT.Identity,
                 scale=bn_scale[:, 0, j : j + 1], bias=bn_shift[:, 0, j : j + 1],
             )
+        a_bfs = {0: first_layer_scalar(0, cos_ps0)}
         cos_sbs[1] = copy_cos(cos_ps1)
+        a_bfs[1] = first_layer_scalar(1, cos_ps1)
 
         w2_codes = const.tile([P, PACK * P], U32, name="w2_codes", align_bytes=64)
         w2_scales = const.tile([P, PACK * P], U8, name="w2_scales", align_bytes=64)
@@ -252,15 +265,16 @@ def tile_p2b_xcorr_pa_kernel(
         )
         fold_bn(1)
 
-        a_bfs = {0: first_layer(0, cos_sbs[0])}
+        first_layer_vector(0, cos_sbs[0], a_bfs[0])
         for unit in range(UNITS):
             grouped = relu_and_group(a_bfs[unit])
             if unit + 1 < UNITS:
-                a_bfs[unit + 1] = first_layer(unit + 1, cos_sbs[unit + 1])
+                first_layer_vector(unit + 1, cos_sbs[unit + 1], a_bfs[unit + 1])
             codes, scales = quantise(grouped)
             if unit + 2 < UNITS:
                 cos_ps = spread_cos(unit + 2)
             accs = second_layer(codes, scales)
             if unit + 2 < UNITS:
                 cos_sbs[unit + 2] = copy_cos(cos_ps)
+                a_bfs[unit + 2] = first_layer_scalar(unit + 2, cos_ps)
             finish(unit, accs)

@@ -40,7 +40,7 @@ def tile_p2b_xcorr_pa_kernel(
         ctx.enter_context(tc.manual_schedule())
         const = ctx.enter_context(tc.tile_pool(name="const", bufs=1))
         work = ctx.enter_context(tc.tile_pool(name="work", bufs=3))
-        store = ctx.enter_context(tc.tile_pool(name="store", bufs=4))
+        store = ctx.enter_context(tc.tile_pool(name="store", bufs=12))
         cos_psum = ctx.enter_context(tc.psum_pool(name="cos_psum", bufs=2))
         acc_psum = ctx.enter_context(tc.psum_pool(name="acc_psum", bufs=6))
 
@@ -140,13 +140,42 @@ def tile_p2b_xcorr_pa_kernel(
             out=rs[:], in0=half_xrr[:], scalar=1.5, in1=r0[:], op0=ALU.add, op1=ALU.mult
         )
 
+        bn_scale = [const.tile([P, PACK], F32, name="bn_scale%d" % layer) for layer in range(2)]
+        bn_mean = [const.tile([P, PACK], F32, name="bn_mean%d" % layer) for layer in range(2)]
+        bn_shift = [const.tile([P, PACK], F32, name="bn_shift%d" % layer) for layer in range(2)]
+
+        def fold_scale(engine, layer):
+            engine.tensor_tensor(
+                out=bn_scale[layer][:], in0=bn_in[:, layer, GAIN, 0:PACK],
+                in1=rs[:, BN0 + layer * PACK : BN0 + (layer + 1) * PACK], op=ALU.mult,
+            )
+
+        def fold_mean(engine, layer):
+            engine.tensor_tensor(
+                out=bn_mean[layer][:], in0=bn_scale[layer][:],
+                in1=bn_in[:, layer, MEAN, 0:PACK], op=ALU.mult,
+            )
+
+        def fold_shift(engine, layer):
+            engine.tensor_tensor(
+                out=bn_shift[layer][:], in0=bn_in[:, layer, SHIFT, 0:PACK],
+                in1=bn_mean[layer][:], op=ALU.subtract,
+            )
+
+        fold_scale(nc.gpsimd, 1)
+        fold_mean(nc.gpsimd, 1)
+        fold_shift(nc.gpsimd, 1)
+
+        fold_scale(nc.vector, 0)
         inv = const.tile([N, M], F32, name="inv")
         nc.vector.tensor_scalar(
             out=inv[:], in0=rs[:, 0:M], scalar1=rs[:, M : M + 1], scalar2=1.0 / COS_EPS,
             op0=ALU.mult, op1=ALU.min,
         )
+        fold_mean(nc.vector, 0)
         cos_t = const.tile([N, M], F32, name="cos_t")
         nc.vector.tensor_tensor(out=cos_t[:], in0=inv[:], in1=dot_ps[:], op=ALU.mult)
+        fold_shift(nc.vector, 0)
 
         def spread_cos(unit):
             cos_ps = cos_psum.tile([P, M_UNIT, N], F32, name="cos_ps", tag="bank")
@@ -215,44 +244,25 @@ def tile_p2b_xcorr_pa_kernel(
             return accs
 
         def finish(unit, accs):
-            result = store.tile([P, PACK, COLS], F32, name="result")
             for j in range(PACK):
+                result = store.tile([P, COLS], F32, name="result")
                 nc.scalar.activation(
-                    out=result[:, j, :], in_=accs[j][:], func=ACT.Relu,
-                    scale=bn_scale[:, 1, j : j + 1], bias=bn_shift[:, 1, j : j + 1],
+                    out=result[:], in_=accs[j][:], func=ACT.Relu,
+                    scale=bn_scale[1][:, j : j + 1], bias=bn_shift[1][:, j : j + 1],
                 )
-            nc.sync.dma_start(out=out_rows[:, :, unit * COLS : (unit + 1) * COLS], in_=result[:])
+                nc.sync.dma_start(out=out_rows[:, j, unit * COLS : (unit + 1) * COLS], in_=result[:])
 
         cos_ps0 = spread_cos(0)
         cos_ps1 = spread_cos(1)
         cos_sbs = {0: copy_cos(cos_ps0)}
 
-        bn_scale = const.tile([P, 2, PACK], F32, name="bn_scale")
-        bn_mean = const.tile([P, 2, PACK], F32, name="bn_mean")
-        bn_shift = const.tile([P, 2, PACK], F32, name="bn_shift")
-
-        def fold_bn(layer):
-            nc.vector.tensor_tensor(
-                out=bn_scale[:, layer, :], in0=bn_in[:, layer, GAIN, 0:PACK],
-                in1=rs[:, BN0 + layer * PACK : BN0 + (layer + 1) * PACK], op=ALU.mult,
-            )
-            nc.vector.tensor_tensor(
-                out=bn_mean[:, layer, :], in0=bn_scale[:, layer, :],
-                in1=bn_in[:, layer, MEAN, 0:PACK], op=ALU.mult,
-            )
-            nc.vector.tensor_tensor(
-                out=bn_shift[:, layer, :], in0=bn_in[:, layer, SHIFT, 0:PACK],
-                in1=bn_mean[:, layer, :], op=ALU.subtract,
-            )
-
-        fold_bn(0)
         c = const.tile([P, PACK], F32, name="c")
-        nc.vector.tensor_tensor(out=c[:], in0=bn_scale[:, 0, :], in1=w1_sb[:, :, 0], op=ALU.mult)
+        nc.vector.tensor_tensor(out=c[:], in0=bn_scale[0][:], in1=w1_sb[:, :, 0], op=ALU.mult)
         base = const.tile([P, PACK, M], F32, name="base")
         for j in range(PACK):
             nc.scalar.activation(
                 out=base[:, j, :], in_=u_ps[:, j, :], func=ACT.Identity,
-                scale=bn_scale[:, 0, j : j + 1], bias=bn_shift[:, 0, j : j + 1],
+                scale=bn_scale[0][:, j : j + 1], bias=bn_shift[0][:, j : j + 1],
             )
         a_bfs = {0: first_layer_scalar(0, cos_ps0)}
         cos_sbs[1] = copy_cos(cos_ps1)
@@ -263,7 +273,6 @@ def tile_p2b_xcorr_pa_kernel(
         nc.vector.quantize_mx(
             out=w2_codes[:].bitcast(FP8X4), scales=w2_scales[:], in_=w2_grouped[:]
         )
-        fold_bn(1)
 
         first_layer_vector(0, cos_sbs[0], a_bfs[0])
         for unit in range(UNITS):

@@ -24,8 +24,20 @@ TINY = 1e-30
 M_UNIT = 4
 COLS = M_UNIT * N
 UNITS = M // M_UNIT
+
+TENSOR_UNITS = 12
+M_TENSOR0 = M - TENSOR_UNITS * M_UNIT
+M_TENSOR = M - M_TENSOR0
+GROUP = 16
+GROUPS = M_TENSOR // GROUP
+SPLIT = 3
+PAIR = 2
+TERMS = SPLIT * SPLIT
+X_ROWS = PAIR * TERMS
+HOT0 = 32
+AHEAD = 3
 PIECES = M_UNIT * PACK
-SCALAR_PIECES = 1
+SCALAR_PIECES = 0
 
 FLOPS = 2 * H * H * M * N + 2 * F * M * N + 2 * H * F * M
 
@@ -39,10 +51,10 @@ def tile_p2b_xcorr_pa_kernel(
     with ExitStack() as ctx:
         ctx.enter_context(tc.manual_schedule())
         const = ctx.enter_context(tc.tile_pool(name="const", bufs=1))
-        work = ctx.enter_context(tc.tile_pool(name="work", bufs=3))
+        work = ctx.enter_context(tc.tile_pool(name="work", bufs=5))
         store = ctx.enter_context(tc.tile_pool(name="store", bufs=12))
-        cos_psum = ctx.enter_context(tc.psum_pool(name="cos_psum", bufs=2))
-        acc_psum = ctx.enter_context(tc.psum_pool(name="acc_psum", bufs=6))
+        cos_psum = ctx.enter_context(tc.psum_pool(name="cos_psum", bufs=4))
+        acc_psum = ctx.enter_context(tc.psum_pool(name="acc_psum", bufs=4))
 
         t_sb = const.tile([F, M], BF16, name="t_sb")
         nc.sync.dma_start(out=t_sb[:], in_=template_feature[0, :, :])
@@ -79,8 +91,34 @@ def tile_p2b_xcorr_pa_kernel(
         warm = const.tile([P, 1], F32, name="warm")
         nc.scalar.activation(out=warm[:], in_=ones[:, 0:1], func=ACT.Abs_reciprocal_sqrt)
 
+        dup = const.tile([N, 2, PAIR, N // 2, PAIR], BF16, name="dup", align_bytes=64)
+        nc.gpsimd.memset(dup[:], 0.0)
+        for h in range(PAIR):
+            nc.gpsimd.tensor_copy(
+                out=dup[:, :, h, :, h], in_=ident_bf[:].rearrange("q (f n) -> q f n", f=2)
+            )
+        x_cols = const.tile([P, 2, M_TENSOR * X_ROWS + P - X_ROWS], BF16, name="x_cols", align_bytes=64)
+        nc.gpsimd.memset(x_cols[:, :, M_TENSOR * X_ROWS :], 0.0)
+        l_cols = const.tile([P, 2, GROUPS, P], BF16, name="l_cols", align_bytes=64)
+        nc.gpsimd.memset(l_cols[:], 0.0)
+        hot_view = ident_bf[:, HOT0:P].rearrange("k (h s i) -> k s i h", h=PAIR, s=SPLIT)
+        hot2 = const.tile([P, GROUP, PAIR], BF16, name="hot2")
+        nc.vector.tensor_tensor(out=hot2[:], in0=hot_view[:, 0], in1=hot_view[:, 1], op=ALU.add)
+        hot = const.tile([P, GROUP, PAIR], BF16, name="hot")
+        nc.vector.tensor_tensor(out=hot[:], in0=hot2[:], in1=hot_view[:, 2], op=ALU.add)
+        moving = const.tile([P, GROUP, N, PAIR], BF16, name="moving", align_bytes=64)
+
+        def fill_moving(first, last):
+            nc.vector.tensor_copy(
+                out=moving[:, first:last, :, :],
+                in_=hot[:, first:last, :].unsqueeze(2).to_broadcast([P, last - first, N, PAIR]),
+            )
+
+        fill_moving(0, GROUP // 2)
+
         t_sq = const.tile([F, M], F32, name="t_sq")
         nc.vector.tensor_tensor(out=t_sq[:], in0=t_sb[:], in1=t_sb[:], op=ALU.mult)
+        fill_moving(GROUP // 2, GROUP)
         s_sq = const.tile([F, N], F32, name="s_sq")
         nc.scalar.activation(out=s_sq[:], in_=s_sb[:], func=ACT.Square)
 
@@ -177,10 +215,10 @@ def tile_p2b_xcorr_pa_kernel(
         nc.vector.tensor_tensor(out=cos_t[:], in0=inv[:], in1=dot_ps[:], op=ALU.mult)
         fold_shift(nc.vector, 0)
 
-        def spread_cos(unit):
+        def spread_cos(m0):
             cos_ps = cos_psum.tile([P, M_UNIT, N], F32, name="cos_ps", tag="bank")
             for i in range(M_UNIT):
-                m = unit * M_UNIT + i
+                m = m0 + i
                 nc.tensor.transpose(
                     cos_ps[:, i, :], cos_t[:, m : m + 1].to_broadcast([N, P]), ident_f32[:]
                 )
@@ -191,21 +229,21 @@ def tile_p2b_xcorr_pa_kernel(
             nc.scalar.copy(out=cos_sb[:], in_=cos_ps[:])
             return cos_sb
 
-        def first_layer_scalar(unit, cos_ps):
+        def first_layer_scalar(m0, cos_ps):
             a_bf = work.tile([P, PACK, COLS], BF16, name="a_bf")
             for piece in range(PIECES - SCALAR_PIECES, PIECES):
                 i, j = divmod(piece, PACK)
-                m = unit * M_UNIT + i
+                m = m0 + i
                 nc.scalar.activation(
                     out=a_bf[:, j, i * N : (i + 1) * N], in_=cos_ps[:, i, :], func=ACT.Identity,
                     scale=c[:, j : j + 1], bias=base[:, j, m : m + 1],
                 )
             return a_bf
 
-        def first_layer_vector(unit, cos_sb, a_bf):
+        def first_layer_vector(m0, cos_sb, a_bf):
             for piece in range(PIECES - SCALAR_PIECES):
                 i, j = divmod(piece, PACK)
-                m = unit * M_UNIT + i
+                m = m0 + i
                 nc.vector.tensor_scalar(
                     out=a_bf[:, j, i * N : (i + 1) * N], in0=cos_sb[:, i, :],
                     scalar1=c[:, j : j + 1], scalar2=base[:, j, m : m + 1],
@@ -243,18 +281,90 @@ def tile_p2b_xcorr_pa_kernel(
                 accs.append(acc)
             return accs
 
-        def finish(unit, accs):
+        def finish(m0, accs):
             for j in range(PACK):
                 result = store.tile([P, COLS], F32, name="result")
                 nc.scalar.activation(
                     out=result[:], in_=accs[j][:], func=ACT.Relu,
                     scale=bn_scale[1][:, j : j + 1], bias=bn_shift[1][:, j : j + 1],
                 )
-                nc.sync.dma_start(out=out_rows[:, j, unit * COLS : (unit + 1) * COLS], in_=result[:])
+                nc.sync.dma_start(out=out_rows[:, j, m0 * N : m0 * N + COLS], in_=result[:])
 
-        cos_ps0 = spread_cos(0)
-        cos_ps1 = spread_cos(1)
-        cos_sbs = {0: copy_cos(cos_ps0)}
+        weights = const.tile([P, 2, GROUPS, P], BF16, name="weights", align_bytes=64)
+
+        def make_weights():
+            w_ps = cos_psum.tile([P, 2, GROUPS, P], BF16, name="w_ps", tag="bank")
+            for pair in range(2):
+                for group in range(GROUPS):
+                    nc.tensor.transpose(w_ps[:, pair, group, :], l_cols[:, pair, group, :], ident_bf[:])
+            nc.scalar.copy(out=weights[:], in_=w_ps[:])
+
+        def cos_rows(m0):
+            x_ps = cos_psum.tile([P, M_UNIT, 2, P], BF16, name="x_ps", tag="bank")
+            for i in range(M_UNIT):
+                first = (m0 - M_TENSOR0 + i) * X_ROWS
+                for half in range(2):
+                    nc.tensor.transpose(
+                        x_ps[:, i, half, :], x_cols[:, half, first : first + P], ident_bf[:]
+                    )
+            slot = (m0 - M_TENSOR0) % GROUP
+            nc.scalar.copy(
+                out=moving[0:HOT0, slot : slot + M_UNIT, :, :].rearrange("k i n h -> k (i n h)"),
+                in_=x_ps[0:HOT0, :, :, :].rearrange("k i f q -> k (i f q)"),
+            )
+
+        def first_layer_tensor(m0):
+            group, slot = divmod(m0 - M_TENSOR0, GROUP)
+            halves = []
+            for first in (slot, slot + 2):
+                a_ps = cos_psum.tile([P, 2 * N, PACK], BF16, name="a_ps", tag="bank")
+                for pair in range(2):
+                    nc.tensor.matmul(
+                        out=a_ps[:, :, PAIR * pair : PAIR * (pair + 1)],
+                        lhsT=weights[:, pair, group, :],
+                        rhs=moving[:, first : first + 2, :, :].rearrange("k i n h -> k (i n) h"),
+                        start=True, stop=True,
+                    )
+                halves.append(a_ps)
+            return halves
+
+        def relu_tensor(halves):
+            grouped = work.tile([P, COLS * PACK], BF16, name="grouped", align_bytes=64)
+            width = 2 * N * PACK
+            for half in range(2):
+                nc.vector.tensor_scalar_max(
+                    out=grouped[:, half * width : (half + 1) * width],
+                    in0=halves[half][:].rearrange("p c t -> p (c t)"), scalar1=0.0,
+                )
+            return grouped
+
+        order = []
+        for position in range(UNITS):
+            tensor_units = sum(1 for m0 in order if m0 >= M_TENSOR0)
+            if position >= 5 and (position - 5) % 9 in (0, 2, 4, 7):
+                order.append(M_TENSOR0 + tensor_units * M_UNIT)
+            else:
+                order.append((position - tensor_units) * M_UNIT)
+
+        def is_tensor(position):
+            return position < UNITS and order[position] >= M_TENSOR0
+
+        def is_vector(position):
+            return position < UNITS and order[position] < M_TENSOR0
+
+        x_parts = const.tile([N, SPLIT, M_TENSOR], BF16, name="x_parts")
+        x_rest = cos_t[:, M_TENSOR0:M]
+        for part in range(SPLIT):
+            nc.vector.tensor_copy(out=x_parts[:, part, :], in_=x_rest)
+            if part < SPLIT - 1:
+                x_next = const.tile([N, M_TENSOR], F32, name="x_next%d" % part)
+                nc.vector.tensor_tensor(
+                    out=x_next[:], in0=x_rest, in1=x_parts[:, part, :], op=ALU.subtract
+                )
+                x_rest = x_next[:]
+
+        cos_pss = [spread_cos(order[position]) for position in range(AHEAD)]
+        cos_sbs = {0: copy_cos(cos_pss[0])}
 
         c = const.tile([P, PACK], F32, name="c")
         nc.vector.tensor_tensor(out=c[:], in0=bn_scale[0][:], in1=w1_sb[:, :, 0], op=ALU.mult)
@@ -264,9 +374,10 @@ def tile_p2b_xcorr_pa_kernel(
                 out=base[:, j, :], in_=u_ps[:, j, :], func=ACT.Identity,
                 scale=bn_scale[0][:, j : j + 1], bias=bn_shift[0][:, j : j + 1],
             )
-        a_bfs = {0: first_layer_scalar(0, cos_ps0)}
-        cos_sbs[1] = copy_cos(cos_ps1)
-        a_bfs[1] = first_layer_scalar(1, cos_ps1)
+        a_bfs = {0: first_layer_scalar(order[0], cos_pss[0])}
+        for position in range(1, AHEAD):
+            cos_sbs[position] = copy_cos(cos_pss[position])
+            a_bfs[position] = first_layer_scalar(order[position], cos_pss[position])
 
         w2_codes = const.tile([P, PACK * P], U32, name="w2_codes", align_bytes=64)
         w2_scales = const.tile([P, PACK * P], U8, name="w2_scales", align_bytes=64)
@@ -274,16 +385,81 @@ def tile_p2b_xcorr_pa_kernel(
             out=w2_codes[:].bitcast(FP8X4), scales=w2_scales[:], in_=w2_grouped[:]
         )
 
-        first_layer_vector(0, cos_sbs[0], a_bfs[0])
-        for unit in range(UNITS):
-            grouped = relu_and_group(a_bfs[unit])
-            if unit + 1 < UNITS:
-                first_layer_vector(unit + 1, cos_sbs[unit + 1], a_bfs[unit + 1])
-            codes, scales = quantise(grouped)
-            if unit + 2 < UNITS:
-                cos_ps = spread_cos(unit + 2)
-            accs = second_layer(codes, scales)
-            if unit + 2 < UNITS:
-                cos_sbs[unit + 2] = copy_cos(cos_ps)
-                a_bfs[unit + 2] = first_layer_scalar(unit + 2, cos_ps)
-            finish(unit, accs)
+        for half in range(2):
+            d_ps = cos_psum.tile([P, PAIR * SPLIT, M_TENSOR], BF16, name="d_ps", tag="bank")
+            for h in range(PAIR):
+                nc.tensor.matmul(
+                    out=d_ps[:, h * SPLIT : (h + 1) * SPLIT, :].rearrange("q x m -> q (x m)"),
+                    lhsT=dup[:, half, h, :, :].rearrange("k n h -> k (n h)"),
+                    rhs=x_parts[:].rearrange("k x m -> k (x m)"),
+                    start=True, stop=True,
+                )
+            nc.scalar.copy(
+                out=x_cols[:, half, 0 : M_TENSOR * X_ROWS].rearrange(
+                    "q (m y w) -> q m y w", y=PAIR * SPLIT, w=SPLIT
+                ),
+                in_=d_ps[:].rearrange("q y m -> q m y").unsqueeze(3).to_broadcast(
+                    [P, M_TENSOR, PAIR * SPLIT, SPLIT]
+                ),
+            )
+
+        c_view = l_cols[:, :, :, 0:X_ROWS].rearrange("p a g (h x w) -> p a g h x w", h=PAIR, x=SPLIT)
+        b_view = l_cols[:, :, :, HOT0:P].rearrange("p a g (h s i) -> p a g h s i", h=PAIR, s=SPLIT)
+        rests = [
+            (
+                base[:, :, M_TENSOR0:M].rearrange("p (a h) (g i) -> p a g h i", a=2, g=GROUPS),
+                c[:].rearrange("p (a h) -> p a h", a=2),
+            )
+        ]
+
+        def write_parts(part):
+            base_rest, c_rest = rests[part]
+            for pair in range(2):
+                nc.scalar.copy(out=b_view[:, pair, :, :, part, :], in_=base_rest[:, pair])
+                nc.scalar.copy(
+                    out=c_view[:, pair, :, :, :, part],
+                    in_=c_rest[:, pair].unsqueeze(1).unsqueeze(3).to_broadcast([P, GROUPS, PAIR, SPLIT]),
+                )
+
+        def subtract_parts(part):
+            base_rest, c_rest = rests[part]
+            base_next = const.tile([P, 2, GROUPS, PAIR, GROUP], F32, name="base_next%d" % part)
+            c_next = const.tile([P, 2, PAIR], F32, name="c_next%d" % part)
+            for pair in range(2):
+                nc.vector.tensor_tensor(
+                    out=base_next[:, pair], in0=base_rest[:, pair],
+                    in1=b_view[:, pair, :, :, part, :], op=ALU.subtract,
+                )
+            nc.vector.tensor_tensor(
+                out=c_next[:], in0=c_rest, in1=c_view[:, :, 0, :, 0, part], op=ALU.subtract
+            )
+            rests.append((base_next[:], c_next[:]))
+
+        write_parts(0)
+        first_layer_vector(order[0], cos_sbs[0], a_bfs[0])
+
+        groups = {}
+        a_tensor = {}
+        for position in range(UNITS):
+            if is_vector(position):
+                groups[position] = relu_and_group(a_bfs[position])
+            if is_vector(position + 1):
+                first_layer_vector(order[position + 1], cos_sbs[position + 1], a_bfs[position + 1])
+            if is_tensor(position + 1):
+                groups[position + 1] = relu_tensor(a_tensor[position + 1])
+            codes, scales = quantise(groups[position])
+            if position < SPLIT - 1:
+                subtract_parts(position)
+            if position == SPLIT - 1:
+                make_weights()
+            if is_vector(position + AHEAD):
+                cos_ps = spread_cos(order[position + AHEAD])
+                cos_sbs[position + AHEAD] = copy_cos(cos_ps)
+                a_bfs[position + AHEAD] = first_layer_scalar(order[position + AHEAD], cos_ps)
+            if is_tensor(position + AHEAD):
+                cos_rows(order[position + AHEAD])
+            if is_tensor(position + 2):
+                a_tensor[position + 2] = first_layer_tensor(order[position + 2])
+            finish(order[position], second_layer(codes, scales))
+            if position < SPLIT - 1:
+                write_parts(position + 1)

@@ -35,7 +35,9 @@ PAIR = 2
 TERMS = SPLIT * SPLIT
 X_ROWS = PAIR * TERMS
 HOT0 = 32
-AHEAD = 3
+AHEAD = 4
+ROWS_AHEAD = 5
+COPY_AHEAD = 4
 PIECES = M_UNIT * PACK
 SCALAR_PIECES = 0
 
@@ -51,9 +53,10 @@ def tile_p2b_xcorr_pa_kernel(
     with ExitStack() as ctx:
         ctx.enter_context(tc.manual_schedule())
         const = ctx.enter_context(tc.tile_pool(name="const", bufs=1))
-        work = ctx.enter_context(tc.tile_pool(name="work", bufs=5))
+        work = ctx.enter_context(tc.tile_pool(name="work", bufs=6))
         store = ctx.enter_context(tc.tile_pool(name="store", bufs=12))
-        cos_psum = ctx.enter_context(tc.psum_pool(name="cos_psum", bufs=4))
+        cos_psum = ctx.enter_context(tc.psum_pool(name="cos_psum", bufs=2))
+        first_psum = ctx.enter_context(tc.psum_pool(name="first_psum", bufs=2))
         acc_psum = ctx.enter_context(tc.psum_pool(name="acc_psum", bufs=4))
 
         t_sb = const.tile([F, M], BF16, name="t_sb")
@@ -293,7 +296,7 @@ def tile_p2b_xcorr_pa_kernel(
         weights = const.tile([P, 2, GROUPS, P], BF16, name="weights", align_bytes=64)
 
         def make_weights():
-            w_ps = cos_psum.tile([P, 2, GROUPS, P], BF16, name="w_ps", tag="bank")
+            w_ps = first_psum.tile([P, 2, GROUPS, P], BF16, name="w_ps", tag="bank")
             for pair in range(2):
                 for group in range(GROUPS):
                     nc.tensor.transpose(w_ps[:, pair, group, :], l_cols[:, pair, group, :], ident_bf[:])
@@ -307,8 +310,11 @@ def tile_p2b_xcorr_pa_kernel(
                     nc.tensor.transpose(
                         x_ps[:, i, half, :], x_cols[:, half, first : first + P], ident_bf[:]
                     )
+            return x_ps
+
+        def copy_rows(m0, x_ps):
             slot = (m0 - M_TENSOR0) % GROUP
-            nc.scalar.copy(
+            nc.vector.tensor_copy(
                 out=moving[0:HOT0, slot : slot + M_UNIT, :, :].rearrange("k i n h -> k (i n h)"),
                 in_=x_ps[0:HOT0, :, :, :].rearrange("k i f q -> k (i f q)"),
             )
@@ -317,7 +323,7 @@ def tile_p2b_xcorr_pa_kernel(
             group, slot = divmod(m0 - M_TENSOR0, GROUP)
             halves = []
             for first in (slot, slot + 2):
-                a_ps = cos_psum.tile([P, 2 * N, PACK], BF16, name="a_ps", tag="bank")
+                a_ps = first_psum.tile([P, 2 * N, PACK], BF16, name="a_ps", tag="bank")
                 for pair in range(2):
                     nc.tensor.matmul(
                         out=a_ps[:, :, PAIR * pair : PAIR * (pair + 1)],
@@ -386,7 +392,7 @@ def tile_p2b_xcorr_pa_kernel(
         )
 
         for half in range(2):
-            d_ps = cos_psum.tile([P, PAIR * SPLIT, M_TENSOR], BF16, name="d_ps", tag="bank")
+            d_ps = first_psum.tile([P, PAIR * SPLIT, M_TENSOR], BF16, name="d_ps", tag="bank")
             for h in range(PAIR):
                 nc.tensor.matmul(
                     out=d_ps[:, h * SPLIT : (h + 1) * SPLIT, :].rearrange("q x m -> q (x m)"),
@@ -440,6 +446,7 @@ def tile_p2b_xcorr_pa_kernel(
 
         groups = {}
         a_tensor = {}
+        x_pss = {}
         for position in range(UNITS):
             if is_vector(position):
                 groups[position] = relu_and_group(a_bfs[position])
@@ -447,19 +454,21 @@ def tile_p2b_xcorr_pa_kernel(
                 first_layer_vector(order[position + 1], cos_sbs[position + 1], a_bfs[position + 1])
             if is_tensor(position + 1):
                 groups[position + 1] = relu_tensor(a_tensor[position + 1])
+            if is_tensor(position + COPY_AHEAD):
+                copy_rows(order[position + COPY_AHEAD], x_pss[position + COPY_AHEAD])
             codes, scales = quantise(groups[position])
             if position < SPLIT - 1:
                 subtract_parts(position)
             if position == SPLIT - 1:
                 make_weights()
+            if is_tensor(position + 2):
+                a_tensor[position + 2] = first_layer_tensor(order[position + 2])
             if is_vector(position + AHEAD):
                 cos_ps = spread_cos(order[position + AHEAD])
                 cos_sbs[position + AHEAD] = copy_cos(cos_ps)
                 a_bfs[position + AHEAD] = first_layer_scalar(order[position + AHEAD], cos_ps)
-            if is_tensor(position + AHEAD):
-                cos_rows(order[position + AHEAD])
-            if is_tensor(position + 2):
-                a_tensor[position + 2] = first_layer_tensor(order[position + 2])
+            if is_tensor(position + ROWS_AHEAD):
+                x_pss[position + ROWS_AHEAD] = cos_rows(order[position + ROWS_AHEAD])
             finish(order[position], second_layer(codes, scales))
             if position < SPLIT - 1:
                 write_parts(position + 1)

@@ -35,11 +35,11 @@ PAIR = 2
 TERMS = SPLIT * SPLIT
 X_ROWS = PAIR * TERMS
 HOT0 = 32
-AHEAD = 4
+TENSOR_SPREAD = 4
+CHUNK = 4
 ROWS_AHEAD = 5
 COPY_AHEAD = 4
 PIECES = M_UNIT * PACK
-SCALAR_PIECES = 0
 
 FLOPS = 2 * H * H * M * N + 2 * F * M * N + 2 * H * F * M
 
@@ -230,21 +230,11 @@ def tile_p2b_xcorr_pa_kernel(
         def copy_cos(cos_ps):
             cos_sb = work.tile([P, M_UNIT, N], F32, name="cos_sb")
             nc.scalar.copy(out=cos_sb[:], in_=cos_ps[:])
-            return cos_sb
+            return cos_sb[:]
 
-        def first_layer_scalar(m0, cos_ps):
+        def first_layer_vector(m0, cos_sb):
             a_bf = work.tile([P, PACK, COLS], BF16, name="a_bf")
-            for piece in range(PIECES - SCALAR_PIECES, PIECES):
-                i, j = divmod(piece, PACK)
-                m = m0 + i
-                nc.scalar.activation(
-                    out=a_bf[:, j, i * N : (i + 1) * N], in_=cos_ps[:, i, :], func=ACT.Identity,
-                    scale=c[:, j : j + 1], bias=base[:, j, m : m + 1],
-                )
-            return a_bf
-
-        def first_layer_vector(m0, cos_sb, a_bf):
-            for piece in range(PIECES - SCALAR_PIECES):
+            for piece in range(PIECES):
                 i, j = divmod(piece, PACK)
                 m = m0 + i
                 nc.vector.tensor_scalar(
@@ -252,6 +242,7 @@ def tile_p2b_xcorr_pa_kernel(
                     scalar1=c[:, j : j + 1], scalar2=base[:, j, m : m + 1],
                     op0=ALU.mult, op1=ALU.add,
                 )
+            return a_bf
 
         def relu_and_group(a_bf):
             grouped = work.tile([P, COLS * PACK], BF16, name="grouped", align_bytes=64)
@@ -284,13 +275,20 @@ def tile_p2b_xcorr_pa_kernel(
                 accs.append(acc)
             return accs
 
-        def finish(m0, accs):
+        def finish(m0, accs, shared):
             for j in range(PACK):
                 result = store.tile([P, COLS], F32, name="result")
-                nc.scalar.activation(
-                    out=result[:], in_=accs[j][:], func=ACT.Relu,
-                    scale=bn_scale[1][:, j : j + 1], bias=bn_shift[1][:, j : j + 1],
-                )
+                if shared and j == PACK - 1:
+                    nc.vector.tensor_scalar(
+                        out=result[:], in0=accs[j][:], scalar1=bn_scale[1][:, j : j + 1],
+                        scalar2=bn_shift[1][:, j : j + 1], op0=ALU.mult, op1=ALU.add,
+                    )
+                    nc.vector.tensor_scalar_max(out=result[:], in0=result[:], scalar1=0.0)
+                else:
+                    nc.scalar.activation(
+                        out=result[:], in_=accs[j][:], func=ACT.Relu,
+                        scale=bn_scale[1][:, j : j + 1], bias=bn_shift[1][:, j : j + 1],
+                    )
                 nc.sync.dma_start(out=out_rows[:, j, m0 * N : m0 * N + COLS], in_=result[:])
 
         weights = const.tile([P, 2, GROUPS, P], BF16, name="weights", align_bytes=64)
@@ -314,7 +312,7 @@ def tile_p2b_xcorr_pa_kernel(
 
         def copy_rows(m0, x_ps):
             slot = (m0 - M_TENSOR0) % GROUP
-            nc.vector.tensor_copy(
+            nc.scalar.copy(
                 out=moving[0:HOT0, slot : slot + M_UNIT, :, :].rearrange("k i n h -> k (i n h)"),
                 in_=x_ps[0:HOT0, :, :, :].rearrange("k i f q -> k (i f q)"),
             )
@@ -347,7 +345,7 @@ def tile_p2b_xcorr_pa_kernel(
         order = []
         for position in range(UNITS):
             tensor_units = sum(1 for m0 in order if m0 >= M_TENSOR0)
-            if position >= 5 and (position - 5) % 9 in (0, 2, 4, 7):
+            if position >= 6 and (position - 6) % 13 in (0, 2, 4, 6, 8, 10):
                 order.append(M_TENSOR0 + tensor_units * M_UNIT)
             else:
                 order.append((position - tensor_units) * M_UNIT)
@@ -358,32 +356,51 @@ def tile_p2b_xcorr_pa_kernel(
         def is_vector(position):
             return position < UNITS and order[position] < M_TENSOR0
 
+        cos_pss = [spread_cos(order[0])]
+        cos_m_ps = cos_psum.tile([M, N], F32, name="cos_m_ps", tag="bank")
+        nc.tensor.transpose(cos_m_ps[:], cos_t[:], ident_f32[:])
+        cos_sbs = {0: copy_cos(cos_pss[0])}
+        for position in range(1, TENSOR_SPREAD):
+            cos_pss.append(spread_cos(order[position]))
+
+        c = const.tile([P, PACK], F32, name="c")
+        nc.vector.tensor_tensor(out=c[:], in0=bn_scale[0][:], in1=w1_sb[:, :, 0], op=ALU.mult)
+        base = const.tile([P, PACK, M], F32, name="base")
+
+        def make_base(j):
+            nc.vector.tensor_scalar(
+                out=base[:, j, :], in0=u_ps[:, j, :], scalar1=bn_scale[0][:, j : j + 1],
+                scalar2=bn_shift[0][:, j : j + 1], op0=ALU.mult, op1=ALU.add,
+            )
+
         x_parts = const.tile([N, SPLIT, M_TENSOR], BF16, name="x_parts")
         x_rest = cos_t[:, M_TENSOR0:M]
         for part in range(SPLIT):
             nc.vector.tensor_copy(out=x_parts[:, part, :], in_=x_rest)
             if part < SPLIT - 1:
+                make_base(2 * part)
                 x_next = const.tile([N, M_TENSOR], F32, name="x_next%d" % part)
                 nc.vector.tensor_tensor(
                     out=x_next[:], in0=x_rest, in1=x_parts[:, part, :], op=ALU.subtract
                 )
+                make_base(2 * part + 1)
                 x_rest = x_next[:]
-
-        cos_pss = [spread_cos(order[position]) for position in range(AHEAD)]
-        cos_sbs = {0: copy_cos(cos_pss[0])}
-
-        c = const.tile([P, PACK], F32, name="c")
-        nc.vector.tensor_tensor(out=c[:], in0=bn_scale[0][:], in1=w1_sb[:, :, 0], op=ALU.mult)
-        base = const.tile([P, PACK, M], F32, name="base")
-        for j in range(PACK):
-            nc.scalar.activation(
-                out=base[:, j, :], in_=u_ps[:, j, :], func=ACT.Identity,
-                scale=bn_scale[0][:, j : j + 1], bias=bn_shift[0][:, j : j + 1],
+        cos_m = const.tile([M, N], F32, name="cos_m")
+        nc.vector.tensor_copy(out=cos_m[:], in_=cos_m_ps[:])
+        spread0 = TENSOR_SPREAD * M_UNIT
+        parked = out[0, H - 1, :, :]
+        nc.sync.dma_start(out=parked[spread0:M_TENSOR0, :], in_=cos_m[spread0:M_TENSOR0, :])
+        for first in range(TENSOR_SPREAD, M_TENSOR0 // M_UNIT, CHUNK):
+            chunk = const.tile([P, CHUNK, M_UNIT, N], F32, name="cos_chunk%d" % first)
+            points = slice(first * M_UNIT, (first + CHUNK) * M_UNIT)
+            nc.sync.dma_start(
+                out=chunk[:].rearrange("p u i n -> p (u i n)"),
+                in_=parked[points, :].rearrange("m n -> (m n)").partition_broadcast(P),
             )
-        a_bfs = {0: first_layer_scalar(order[0], cos_pss[0])}
-        for position in range(1, AHEAD):
+            for unit in range(first, first + CHUNK):
+                cos_sbs[order.index(unit * M_UNIT)] = chunk[:, unit - first, :, :]
+        for position in range(1, TENSOR_SPREAD):
             cos_sbs[position] = copy_cos(cos_pss[position])
-            a_bfs[position] = first_layer_scalar(order[position], cos_pss[position])
 
         w2_codes = const.tile([P, PACK * P], U32, name="w2_codes", align_bytes=64)
         w2_scales = const.tile([P, PACK * P], U8, name="w2_scales", align_bytes=64)
@@ -442,7 +459,7 @@ def tile_p2b_xcorr_pa_kernel(
             rests.append((base_next[:], c_next[:]))
 
         write_parts(0)
-        first_layer_vector(order[0], cos_sbs[0], a_bfs[0])
+        a_bfs = {0: first_layer_vector(order[0], cos_sbs[0])}
 
         groups = {}
         a_tensor = {}
@@ -450,25 +467,24 @@ def tile_p2b_xcorr_pa_kernel(
         for position in range(UNITS):
             if is_vector(position):
                 groups[position] = relu_and_group(a_bfs[position])
+            if position == 0:
+                codes, scales = quantise(groups[position])
             if is_vector(position + 1):
-                first_layer_vector(order[position + 1], cos_sbs[position + 1], a_bfs[position + 1])
+                a_bfs[position + 1] = first_layer_vector(order[position + 1], cos_sbs[position + 1])
             if is_tensor(position + 1):
                 groups[position + 1] = relu_tensor(a_tensor[position + 1])
             if is_tensor(position + COPY_AHEAD):
                 copy_rows(order[position + COPY_AHEAD], x_pss[position + COPY_AHEAD])
-            codes, scales = quantise(groups[position])
+            if position > 0:
+                codes, scales = quantise(groups[position])
             if position < SPLIT - 1:
                 subtract_parts(position)
-            if position == SPLIT - 1:
-                make_weights()
             if is_tensor(position + 2):
                 a_tensor[position + 2] = first_layer_tensor(order[position + 2])
-            if is_vector(position + AHEAD):
-                cos_ps = spread_cos(order[position + AHEAD])
-                cos_sbs[position + AHEAD] = copy_cos(cos_ps)
-                a_bfs[position + AHEAD] = first_layer_scalar(order[position + AHEAD], cos_ps)
             if is_tensor(position + ROWS_AHEAD):
                 x_pss[position + ROWS_AHEAD] = cos_rows(order[position + ROWS_AHEAD])
-            finish(order[position], second_layer(codes, scales))
+            finish(order[position], second_layer(codes, scales), position == UNITS - 1)
             if position < SPLIT - 1:
                 write_parts(position + 1)
+            if position == SPLIT - 1:
+                make_weights()

from contextlib import ExitStack

import concourse.mybir as mybir
from concourse.masks import make_identity

F32 = mybir.dt.float32
BF16 = mybir.dt.bfloat16
U32 = mybir.dt.uint32
U8 = mybir.dt.uint8
FP8X4 = mybir.dt.float8_e4m3fn_x4
ALU = mybir.AluOpType
ACT = mybir.ActivationFunctionType

P = 128
PACK = 4
F = 128
M = 128
N = 128
H = P * PACK
BN_EPS = 1e-5
COS_EPS = 1e-8
TINY = 1e-30

M_UNIT = 4
COLS = M_UNIT * N
UNITS = M // M_UNIT

TENSOR_UNITS = 12
M_TENSOR0 = M - TENSOR_UNITS * M_UNIT
M_TENSOR = M - M_TENSOR0
GROUP = 16
GROUPS = M_TENSOR // GROUP
SPLIT = 3
PAIR = 2
TERMS = SPLIT * SPLIT
X_ROWS = PAIR * TERMS
HOT0 = 32
TENSOR_SPREAD = 4
CHUNK = 4
ROWS_AHEAD = 5
COPY_AHEAD = 4
PIECES = M_UNIT * PACK

FLOPS = 2 * H * H * M * N + 2 * F * M * N + 2 * H * F * M


def tile_p2b_xcorr_pa_kernel(
    tc, template_feature, search_feature, W1, W2, g1, b1, m1, v1, g2, b2, m2, v2, out
):
    nc = tc.nc
    out_rows = out[0, :, :, :].rearrange("(p j) m n -> p j (m n)", j=PACK)

    with ExitStack() as ctx:
        ctx.enter_context(tc.manual_schedule())
        const = ctx.enter_context(tc.tile_pool(name="const", bufs=1))
        work = ctx.enter_context(tc.tile_pool(name="work", bufs=6))
        store = ctx.enter_context(tc.tile_pool(name="store", bufs=12))
        cos_psum = ctx.enter_context(tc.psum_pool(name="cos_psum", bufs=2))
        first_psum = ctx.enter_context(tc.psum_pool(name="first_psum", bufs=2))
        acc_psum = ctx.enter_context(tc.psum_pool(name="acc_psum", bufs=4))

        t_sb = const.tile([F, M], BF16, name="t_sb")
        nc.sync.dma_start(out=t_sb[:], in_=template_feature[0, :, :])
        s_sb = const.tile([F, N], BF16, name="s_sb")
        nc.scalar.dma_start(out=s_sb[:], in_=search_feature[0, :, :])
        w2_sb = const.tile([P, PACK * H], BF16, name="w2_sb")
        nc.scalar.dma_start(out=w2_sb[:], in_=W2.rearrange("(p j) h -> p (j h)", j=PACK))

        VAR, GAIN, MEAN, SHIFT = 0, 1, 2, 3
        bn_in = const.tile([P, 2, 4, 16], BF16, name="bn_in")

        def load_bn(vector, layer, kind):
            nc.sync.dma_start(
                out=bn_in[:, layer, kind, 0:PACK], in_=vector.rearrange("(p j) -> p j", j=PACK)
            )

        load_bn(v1, 0, VAR)
        load_bn(v2, 1, VAR)
        w1_sb = const.tile([P, PACK, F + 1], BF16, name="w1_sb")
        nc.sync.dma_start(out=w1_sb[:], in_=W1.rearrange("(p j) c -> p j c", j=PACK))
        load_bn(g1, 0, GAIN)
        load_bn(m1, 0, MEAN)
        load_bn(b1, 0, SHIFT)
        load_bn(g2, 1, GAIN)
        load_bn(m2, 1, MEAN)
        load_bn(b2, 1, SHIFT)

        ident_bf = const.tile([P, P], BF16, name="ident_bf")
        make_identity(nc, ident_bf[:])
        ident_f32 = const.tile([P, P], F32, name="ident_f32")
        make_identity(nc, ident_f32[:])
        ones = const.tile([P, P], F32, name="ones")
        nc.vector.memset(ones[:], 1.0)
        warm = const.tile([P, 1], F32, name="warm")
        nc.scalar.activation(out=warm[:], in_=ones[:, 0:1], func=ACT.Abs_reciprocal_sqrt)

        dup = const.tile([N, 2, PAIR, N // 2, PAIR], BF16, name="dup", align_bytes=64)
        nc.gpsimd.memset(dup[:], 0.0)
        for h in range(PAIR):
            nc.gpsimd.tensor_copy(
                out=dup[:, :, h, :, h], in_=ident_bf[:].rearrange("q (f n) -> q f n", f=2)
            )
        x_cols = const.tile([P, 2, M_TENSOR * X_ROWS + P - X_ROWS], BF16, name="x_cols", align_bytes=64)
        nc.gpsimd.memset(x_cols[:, :, M_TENSOR * X_ROWS :], 0.0)
        l_cols = const.tile([P, 2, GROUPS, P], BF16, name="l_cols", align_bytes=64)
        nc.gpsimd.memset(l_cols[:], 0.0)
        hot_view = ident_bf[:, HOT0:P].rearrange("k (h s i) -> k s i h", h=PAIR, s=SPLIT)
        hot2 = const.tile([P, GROUP, PAIR], BF16, name="hot2")
        nc.vector.tensor_tensor(out=hot2[:], in0=hot_view[:, 0], in1=hot_view[:, 1], op=ALU.add)
        hot = const.tile([P, GROUP, PAIR], BF16, name="hot")
        nc.vector.tensor_tensor(out=hot[:], in0=hot2[:], in1=hot_view[:, 2], op=ALU.add)
        moving = const.tile([P, GROUP, N, PAIR], BF16, name="moving", align_bytes=64)

        def fill_moving(first, last):
            nc.vector.tensor_copy(
                out=moving[:, first:last, :, :],
                in_=hot[:, first:last, :].unsqueeze(2).to_broadcast([P, last - first, N, PAIR]),
            )

        fill_moving(0, GROUP // 2)

        t_sq = const.tile([F, M], F32, name="t_sq")
        nc.vector.tensor_tensor(out=t_sq[:], in0=t_sb[:], in1=t_sb[:], op=ALU.mult)
        fill_moving(GROUP // 2, GROUP)
        s_sq = const.tile([F, N], F32, name="s_sq")
        nc.scalar.activation(out=s_sq[:], in_=s_sb[:], func=ACT.Square)

        dot_ps = cos_psum.tile([N, M], F32, name="dot_ps", tag="bank")
        nc.tensor.matmul(out=dot_ps[:], lhsT=s_sb[:], rhs=t_sb[:], start=True, stop=True)
        norm_ps = cos_psum.tile([N, M + 1], F32, name="norm_ps", tag="bank")
        nc.tensor.matmul(out=norm_ps[:, 0:M], lhsT=ones[:], rhs=t_sq[:], start=True, stop=True)
        nc.tensor.matmul(
            out=norm_ps[:, M : M + 1], lhsT=s_sq[:], rhs=ones[:, 0:1], start=True, stop=True
        )

        BN0 = M + 1
        ROOTS = BN0 + 2 * PACK
        x = const.tile([P, ROOTS], F32, name="x")
        nc.vector.tensor_scalar_max(out=x[:, 0:BN0], in0=norm_ps[:], scalar1=TINY)
        nc.vector.tensor_scalar_add(
            out=x[:, BN0:ROOTS].rearrange("p (l j) -> p l j", j=PACK),
            in0=bn_in[:, :, VAR, 0:PACK],
            scalar1=BN_EPS,
        )
        r0 = const.tile([P, ROOTS], F32, name="r0")
        nc.scalar.activation(out=r0[:], in_=x[:], func=ACT.Abs_reciprocal_sqrt)

        w1t_ps = acc_psum.tile([F, PACK, P], BF16, name="w1t_ps", tag="bank")
        for j in range(PACK):
            nc.tensor.transpose(w1t_ps[:, j, :], w1_sb[:, j, 1 : F + 1], ident_bf[:])
        w1t = const.tile([F, PACK, P], BF16, name="w1t")
        nc.scalar.copy(out=w1t[:], in_=w1t_ps[:])

        w2_words = w2_sb[:].bitcast(F32).rearrange("p (j q u) -> p j u q", j=PACK, u=2)
        w2_grouped = const.tile([P, PACK * P * PACK], BF16, name="w2_grouped", align_bytes=64)
        w2_grouped_words = w2_grouped[:].bitcast(F32).rearrange("p (j g u) -> p j g u", j=PACK, u=2)
        for half in range(2):
            w2t_ps = acc_psum.tile([P, 2, 2, P], F32, name="w2t_ps", tag="bank")
            for jj in range(2):
                for u in range(2):
                    nc.tensor.transpose(
                        w2t_ps[:, jj, u, :], w2_words[:, 2 * half + jj, u, :], ident_f32[:]
                    )
            nc.scalar.copy(
                out=w2_grouped_words[:, 2 * half : 2 * half + 2, :, :],
                in_=w2t_ps[:].rearrange("p j u g -> p j g u"),
            )

        u_ps = acc_psum.tile([P, PACK, M], F32, name="u_ps", tag="bank")
        for j in range(PACK):
            nc.tensor.matmul(out=u_ps[:, j, :], lhsT=w1t[:, j, :], rhs=t_sb[:], start=True, stop=True)

        xr = const.tile([P, ROOTS], F32, name="xr")
        nc.vector.tensor_tensor(out=xr[:], in0=x[:], in1=r0[:], op=ALU.mult)
        half_xrr = const.tile([P, ROOTS], F32, name="half_xrr")
        nc.vector.scalar_tensor_tensor(
            out=half_xrr[:], in0=xr[:], scalar=-0.5, in1=r0[:], op0=ALU.mult, op1=ALU.mult
        )
        rs = const.tile([P, ROOTS], F32, name="rs")
        nc.vector.scalar_tensor_tensor(
            out=rs[:], in0=half_xrr[:], scalar=1.5, in1=r0[:], op0=ALU.add, op1=ALU.mult
        )

        bn_scale = [const.tile([P, PACK], F32, name="bn_scale%d" % layer) for layer in range(2)]
        bn_mean = [const.tile([P, PACK], F32, name="bn_mean%d" % layer) for layer in range(2)]
        bn_shift = [const.tile([P, PACK], F32, name="bn_shift%d" % layer) for layer in range(2)]

        def fold_scale(engine, layer):
            engine.tensor_tensor(
                out=bn_scale[layer][:], in0=bn_in[:, layer, GAIN, 0:PACK],
                in1=rs[:, BN0 + layer * PACK : BN0 + (layer + 1) * PACK], op=ALU.mult,
            )

        def fold_mean(engine, layer):
            engine.tensor_tensor(
                out=bn_mean[layer][:], in0=bn_scale[layer][:],
                in1=bn_in[:, layer, MEAN, 0:PACK], op=ALU.mult,
            )

        def fold_shift(engine, layer):
            engine.tensor_tensor(
                out=bn_shift[layer][:], in0=bn_in[:, layer, SHIFT, 0:PACK],
                in1=bn_mean[layer][:], op=ALU.subtract,
            )

        fold_scale(nc.gpsimd, 1)
        fold_mean(nc.gpsimd, 1)
        fold_shift(nc.gpsimd, 1)

        fold_scale(nc.vector, 0)
        inv = const.tile([N, M], F32, name="inv")
        nc.vector.tensor_scalar(
            out=inv[:], in0=rs[:, 0:M], scalar1=rs[:, M : M + 1], scalar2=1.0 / COS_EPS,
            op0=ALU.mult, op1=ALU.min,
        )
        fold_mean(nc.vector, 0)
        cos_t = const.tile([N, M], F32, name="cos_t")
        nc.vector.tensor_tensor(out=cos_t[:], in0=inv[:], in1=dot_ps[:], op=ALU.mult)
        fold_shift(nc.vector, 0)

        def spread_cos(m0):
            cos_ps = cos_psum.tile([P, M_UNIT, N], F32, name="cos_ps", tag="bank")
            for i in range(M_UNIT):
                m = m0 + i
                nc.tensor.transpose(
                    cos_ps[:, i, :], cos_t[:, m : m + 1].to_broadcast([N, P]), ident_f32[:]
                )
            return cos_ps

        def copy_cos(cos_ps):
            cos_sb = work.tile([P, M_UNIT, N], F32, name="cos_sb")
            nc.scalar.copy(out=cos_sb[:], in_=cos_ps[:])
            return cos_sb[:]

        def first_layer_vector(m0, cos_sb):
            a_bf = work.tile([P, PACK, COLS], BF16, name="a_bf")
            for piece in range(PIECES):
                i, j = divmod(piece, PACK)
                m = m0 + i
                nc.vector.tensor_scalar(
                    out=a_bf[:, j, i * N : (i + 1) * N], in0=cos_sb[:, i, :],
                    scalar1=c[:, j : j + 1], scalar2=base[:, j, m : m + 1],
                    op0=ALU.mult, op1=ALU.add,
                )
            return a_bf

        def relu_and_group(a_bf):
            grouped = work.tile([P, COLS * PACK], BF16, name="grouped", align_bytes=64)
            nc.vector.tensor_scalar_max(
                out=grouped[:].rearrange("p (c i t) -> p c t i", i=4, t=PACK),
                in0=a_bf[:].rearrange("p t (c i) -> p c t i", i=4),
                scalar1=0.0,
            )
            return grouped

        def quantise(grouped):
            codes = work.tile([P, COLS], U32, name="codes", align_bytes=64)
            scales = work.tile([P, COLS], U8, name="scales", align_bytes=64)
            nc.vector.quantize_mx(out=codes[:].bitcast(FP8X4), scales=scales[:], in_=grouped[:])
            return codes, scales

        def second_layer(codes, scales):
            accs = []
            for j in range(PACK):
                acc = acc_psum.tile([P, COLS], F32, name="acc", tag="bank")
                nc.tensor.matmul_mx(
                    out=acc[:],
                    lhsT=w2_codes[:, j * P : (j + 1) * P].bitcast(FP8X4),
                    lhsT_scale=w2_scales[:, j * P : (j + 1) * P],
                    rhs=codes[:].bitcast(FP8X4),
                    rhs_scale=scales[:],
                    start=True,
                    stop=True,
                )
                accs.append(acc)
            return accs

        def finish(m0, accs, shared):
            for j in range(PACK):
                result = store.tile([P, COLS], F32, name="result")
                if shared and j == PACK - 1:
                    nc.vector.tensor_scalar(
                        out=result[:], in0=accs[j][:], scalar1=bn_scale[1][:, j : j + 1],
                        scalar2=bn_shift[1][:, j : j + 1], op0=ALU.mult, op1=ALU.add,
                    )
                    nc.vector.tensor_scalar_max(out=result[:], in0=result[:], scalar1=0.0)
                else:
                    nc.scalar.activation(
                        out=result[:], in_=accs[j][:], func=ACT.Relu,
                        scale=bn_scale[1][:, j : j + 1], bias=bn_shift[1][:, j : j + 1],
                    )
                nc.sync.dma_start(out=out_rows[:, j, m0 * N : m0 * N + COLS], in_=result[:])

        weights = const.tile([P, 2, GROUPS, P], BF16, name="weights", align_bytes=64)

        def make_weights():
            w_ps = first_psum.tile([P, 2, GROUPS, P], BF16, name="w_ps", tag="bank")
            for pair in range(2):
                for group in range(GROUPS):
                    nc.tensor.transpose(w_ps[:, pair, group, :], l_cols[:, pair, group, :], ident_bf[:])
            nc.scalar.copy(out=weights[:], in_=w_ps[:])

        def cos_rows(m0):
            x_ps = cos_psum.tile([P, M_UNIT, 2, P], BF16, name="x_ps", tag="bank")
            for i in range(M_UNIT):
                first = (m0 - M_TENSOR0 + i) * X_ROWS
                for half in range(2):
                    nc.tensor.transpose(
                        x_ps[:, i, half, :], x_cols[:, half, first : first + P], ident_bf[:]
                    )
            return x_ps

        def copy_rows(m0, x_ps):
            slot = (m0 - M_TENSOR0) % GROUP
            nc.scalar.copy(
                out=moving[0:HOT0, slot : slot + M_UNIT, :, :].rearrange("k i n h -> k (i n h)"),
                in_=x_ps[0:HOT0, :, :, :].rearrange("k i f q -> k (i f q)"),
            )

        def first_layer_tensor(m0):
            group, slot = divmod(m0 - M_TENSOR0, GROUP)
            halves = []
            for first in (slot, slot + 2):
                a_ps = first_psum.tile([P, 2 * N, PACK], BF16, name="a_ps", tag="bank")
                for pair in range(2):
                    nc.tensor.matmul(
                        out=a_ps[:, :, PAIR * pair : PAIR * (pair + 1)],
                        lhsT=weights[:, pair, group, :],
                        rhs=moving[:, first : first + 2, :, :].rearrange("k i n h -> k (i n) h"),
                        start=True, stop=True,
                    )
                halves.append(a_ps)
            return halves

        def relu_tensor(halves):
            grouped = work.tile([P, COLS * PACK], BF16, name="grouped", align_bytes=64)
            width = 2 * N * PACK
            for half in range(2):
                nc.vector.tensor_scalar_max(
                    out=grouped[:, half * width : (half + 1) * width],
                    in0=halves[half][:].rearrange("p c t -> p (c t)"), scalar1=0.0,
                )
            return grouped

        order = []
        for position in range(UNITS):
            tensor_units = sum(1 for m0 in order if m0 >= M_TENSOR0)
            if position >= 6 and (position - 6) % 13 in (0, 2, 4, 6, 8, 10):
                order.append(M_TENSOR0 + tensor_units * M_UNIT)
            else:
                order.append((position - tensor_units) * M_UNIT)

        def is_tensor(position):
            return position < UNITS and order[position] >= M_TENSOR0

        def is_vector(position):
            return position < UNITS and order[position] < M_TENSOR0

        cos_pss = [spread_cos(order[0])]
        cos_m_ps = cos_psum.tile([M, N], F32, name="cos_m_ps", tag="bank")
        nc.tensor.transpose(cos_m_ps[:], cos_t[:], ident_f32[:])
        cos_sbs = {0: copy_cos(cos_pss[0])}
        for position in range(1, TENSOR_SPREAD):
            cos_pss.append(spread_cos(order[position]))

        c = const.tile([P, PACK], F32, name="c")
        nc.vector.tensor_tensor(out=c[:], in0=bn_scale[0][:], in1=w1_sb[:, :, 0], op=ALU.mult)
        base = const.tile([P, PACK, M], F32, name="base")

        def make_base(j):
            nc.vector.tensor_scalar(
                out=base[:, j, :], in0=u_ps[:, j, :], scalar1=bn_scale[0][:, j : j + 1],
                scalar2=bn_shift[0][:, j : j + 1], op0=ALU.mult, op1=ALU.add,
            )

        x_parts = const.tile([N, SPLIT, M_TENSOR], BF16, name="x_parts")
        x_rest = cos_t[:, M_TENSOR0:M]
        for part in range(SPLIT):
            nc.vector.tensor_copy(out=x_parts[:, part, :], in_=x_rest)
            if part < SPLIT - 1:
                make_base(2 * part)
                x_next = const.tile([N, M_TENSOR], F32, name="x_next%d" % part)
                nc.vector.tensor_tensor(
                    out=x_next[:], in0=x_rest, in1=x_parts[:, part, :], op=ALU.subtract
                )
                make_base(2 * part + 1)
                x_rest = x_next[:]
        cos_m = const.tile([M, N], F32, name="cos_m")
        nc.vector.tensor_copy(out=cos_m[:], in_=cos_m_ps[:])
        spread0 = TENSOR_SPREAD * M_UNIT
        parked = out[0, H - 1, :, :]
        nc.sync.dma_start(out=parked[spread0:M_TENSOR0, :], in_=cos_m[spread0:M_TENSOR0, :])
        for first in range(TENSOR_SPREAD, M_TENSOR0 // M_UNIT, CHUNK):
            chunk = const.tile([P, CHUNK, M_UNIT, N], F32, name="cos_chunk%d" % first)
            points = slice(first * M_UNIT, (first + CHUNK) * M_UNIT)
            nc.sync.dma_start(
                out=chunk[:].rearrange("p u i n -> p (u i n)"),
                in_=parked[points, :].rearrange("m n -> (m n)").partition_broadcast(P),
            )
            for unit in range(first, first + CHUNK):
                cos_sbs[order.index(unit * M_UNIT)] = chunk[:, unit - first, :, :]
        for position in range(1, TENSOR_SPREAD):
            cos_sbs[position] = copy_cos(cos_pss[position])

        w2_codes = const.tile([P, PACK * P], U32, name="w2_codes", align_bytes=64)
        w2_scales = const.tile([P, PACK * P], U8, name="w2_scales", align_bytes=64)
        nc.vector.quantize_mx(
            out=w2_codes[:].bitcast(FP8X4), scales=w2_scales[:], in_=w2_grouped[:]
        )

        for half in range(2):
            d_ps = first_psum.tile([P, PAIR * SPLIT, M_TENSOR], BF16, name="d_ps", tag="bank")
            for h in range(PAIR):
                nc.tensor.matmul(
                    out=d_ps[:, h * SPLIT : (h + 1) * SPLIT, :].rearrange("q x m -> q (x m)"),
                    lhsT=dup[:, half, h, :, :].rearrange("k n h -> k (n h)"),
                    rhs=x_parts[:].rearrange("k x m -> k (x m)"),
                    start=True, stop=True,
                )
            nc.scalar.copy(
                out=x_cols[:, half, 0 : M_TENSOR * X_ROWS].rearrange(
                    "q (m y w) -> q m y w", y=PAIR * SPLIT, w=SPLIT
                ),
                in_=d_ps[:].rearrange("q y m -> q m y").unsqueeze(3).to_broadcast(
                    [P, M_TENSOR, PAIR * SPLIT, SPLIT]
                ),
            )

        c_view = l_cols[:, :, :, 0:X_ROWS].rearrange("p a g (h x w) -> p a g h x w", h=PAIR, x=SPLIT)
        b_view = l_cols[:, :, :, HOT0:P].rearrange("p a g (h s i) -> p a g h s i", h=PAIR, s=SPLIT)
        rests = [
            (
                base[:, :, M_TENSOR0:M].rearrange("p (a h) (g i) -> p a g h i", a=2, g=GROUPS),
                c[:].rearrange("p (a h) -> p a h", a=2),
            )
        ]

        def write_parts(part):
            base_rest, c_rest = rests[part]
            for pair in range(2):
                nc.scalar.copy(out=b_view[:, pair, :, :, part, :], in_=base_rest[:, pair])
                nc.scalar.copy(
                    out=c_view[:, pair, :, :, :, part],
                    in_=c_rest[:, pair].unsqueeze(1).unsqueeze(3).to_broadcast([P, GROUPS, PAIR, SPLIT]),
                )

        def subtract_parts(part):
            base_rest, c_rest = rests[part]
            base_next = const.tile([P, 2, GROUPS, PAIR, GROUP], F32, name="base_next%d" % part)
            c_next = const.tile([P, 2, PAIR], F32, name="c_next%d" % part)
            for pair in range(2):
                nc.vector.tensor_tensor(
                    out=base_next[:, pair], in0=base_rest[:, pair],
                    in1=b_view[:, pair, :, :, part, :], op=ALU.subtract,
                )
            nc.vector.tensor_tensor(
                out=c_next[:], in0=c_rest, in1=c_view[:, :, 0, :, 0, part], op=ALU.subtract
            )
            rests.append((base_next[:], c_next[:]))

        write_parts(0)
        a_bfs = {0: first_layer_vector(order[0], cos_sbs[0])}

        groups = {}
        a_tensor = {}
        x_pss = {}
        for position in range(UNITS):
            if is_vector(position):
                groups[position] = relu_and_group(a_bfs[position])
            if position == 0:
                codes, scales = quantise(groups[position])
            if is_vector(position + 1):
                a_bfs[position + 1] = first_layer_vector(order[position + 1], cos_sbs[position + 1])
            if is_tensor(position + 1):
                groups[position + 1] = relu_tensor(a_tensor[position + 1])
            if is_tensor(position + COPY_AHEAD):
                copy_rows(order[position + COPY_AHEAD], x_pss[position + COPY_AHEAD])
            if position > 0:
                codes, scales = quantise(groups[position])
            if position < SPLIT - 1:
                subtract_parts(position)
            if is_tensor(position + 2):
                a_tensor[position + 2] = first_layer_tensor(order[position + 2])
            if is_tensor(position + ROWS_AHEAD):
                x_pss[position + ROWS_AHEAD] = cos_rows(order[position + ROWS_AHEAD])
            finish(order[position], second_layer(codes, scales), position == UNITS - 1)
            if position < SPLIT - 1:
                write_parts(position + 1)
            if position == SPLIT - 1:
                make_weights()
